import numpy as np
import ml_dtypes


def mxq(x, axis, fmt="e4m3"):
    dtype, down = {"e4m3": (ml_dtypes.float8_e4m3fn, 7), "e5m2": (ml_dtypes.float8_e5m2, 14)}[fmt]
    v = np.moveaxis(np.asarray(x, np.float32).astype(ml_dtypes.bfloat16).astype(np.float64), axis, -1)
    blocks = v.reshape(v.shape[:-1] + (-1, 32))
    amax = np.abs(blocks).max(-1, keepdims=True)
    byte = np.maximum(np.where(amax > 0, np.frexp(amax)[1] - 1 + 127, 0) - down, 1)
    scale = np.exp2(byte - 127.0)
    codes = (blocks / scale).astype(np.float32).astype(dtype).astype(np.float64)
    return np.moveaxis((codes * scale).reshape(v.shape), -1, axis)


WIDE = False


def mx_kscale(k):
    if not WIDE:
        return np.ones(k)
    levels = np.array([10, -10, 5, -5, 0])
    a = np.random.permutation(np.resize(levels, k // 512 * 4)).reshape(k // 512, 4)
    idx = np.arange(k)
    return np.exp2(a[idx // 512, idx % 128 // 32])


BF16 = ml_dtypes.bfloat16


def bf(x):
    return np.asarray(x, np.float32).astype(BF16)


def f64(x):
    return np.asarray(x).astype(np.float64)


B, N, C = 1, 2048, 512
Q = N ** 0.25


def setup_inputs():
    s = mx_kscale(N)
    msg = (1.4 * np.random.standard_normal((B, 1, C)) + 1.2 * np.random.standard_normal((B, N, C))) / Q
    return {"A": bf(np.random.uniform(0.0, 1.0, (B, N, N)) * 2.0 / N ** 0.75 * s),
            "msg": bf(msg / s[:, None]),
            "h": bf(np.maximum(np.random.standard_normal((B, N, C)) * 1.35, 0.0)),
            "Ws": bf(np.random.uniform(-1.0, 1.0, (C, C)) * 1.5 / np.sqrt(C)),
            "b": bf(np.random.uniform(-1.0, 1.0, C) * 0.5)}


def reference(A, msg, h, Ws, b):
    agg = mxq(f64(A), 2, "e4m3") @ mxq(f64(msg), 1, "e4m3")
    return np.maximum(agg + f64(h) @ f64(Ws).T + f64(b), 0.0)

@@ -1,0 +1,302 @@
+from contextlib import ExitStack
+
+import concourse.masks as masks
+import concourse.mybir as mybir
+
+F32 = mybir.dt.float32
+BF16 = mybir.dt.bfloat16
+U32 = mybir.dt.uint32
+U8 = mybir.dt.uint8
+FP8X4 = mybir.dt.float8_e4m3fn_x4
+ADD = mybir.AluOpType.add
+RELU = mybir.ActivationFunctionType.Relu
+
+P = 128
+NODES = 2048
+C = 512
+NT = NODES // P
+NG = NODES // 512
+FLOPS = 2 * NODES * NODES * C + 2 * NODES * C * C
+
+LA = 4
+LM = 6
+A_BUFS = 10
+
+
+def tile_gcnstacking_pb_kernel(tc, A, msg, h, Ws, b, out):
+    nc = tc.nc
+    a_view = A.rearrange("b (p t) j -> p (b t) j", t=NT)
+    h_view = h.rearrange("b (p t) k -> p (b t) k", t=NT)
+    o_view = out.rearrange("b (p t) c -> p (b t) c", t=NT)
+    m_view = msg.rearrange("b (s p e) c -> p (b s) (e c)", s=2 * NG, p=P, e=2)
+    w_view = Ws.rearrange("(o p) k -> p o k", p=P)
+    b_view = b.rearrange("(o c) -> o c", o=1)
+
+    with ExitStack() as ctx:
+        keep = ctx.enter_context(tc.tile_pool(name="keep", bufs=1))
+        a_pool = ctx.enter_context(tc.tile_pool(name="araw", bufs=A_BUFS))
+        g_pool = ctx.enter_context(tc.tile_pool(name="agrp", bufs=3))
+        ps_t = ctx.enter_context(tc.psum_pool(name="pst", bufs=3))
+        ps_s = ctx.enter_context(tc.psum_pool(name="pss", bufs=3))
+        ps_a = ctx.enter_context(tc.psum_pool(name="psa", bufs=2))
+        ctx.enter_context(tc.manual_schedule())
+
+        ident = keep.tile([P, P], F32, name="ident")
+        masks.make_identity(nc, ident[:])
+        ones = keep.tile([P, P], BF16, name="ones")
+        nc.vector.memset(ones[:], 1.0)
+        brow = keep.tile([P, C], BF16, name="brow")
+        nc.vector.memset(brow[:], 0.0)
+        warm = keep.tile([P, 1], F32, name="warm")
+        nc.vector.memset(warm[:], 0.0)
+        nc.scalar.dma_start(out=brow[0:1, :], in_=b_view)
+        nc.scalar.activation(out=warm[:], in_=warm[:], func=RELU)
+
+        a_sb = {}
+        h_sb = {}
+        m_raw = {}
+
+        def load_a(t):
+            a_sb[t] = a_pool.tile([P, NODES], BF16, name="a%d" % t, tag="a")
+            nc.sync.dma_start(out=a_sb[t][:], in_=a_view[:, t, :])
+
+        def load_h(q):
+            h_sb[q] = keep.tile([P, 4, C], BF16, name="h%d" % q)
+            nc.sync.dma_start(out=h_sb[q][:], in_=h_view[:, 4 * q : 4 * q + 4, :])
+
+        def load_m(g):
+            m_raw[g] = keep.tile([P, 2, 2 * C], BF16, name="mraw%d" % g)
+            nc.sync.dma_start(out=m_raw[g][:], in_=m_view[:, 2 * g : 2 * g + 2, :])
+
+        ws_sb = keep.tile([P, 4, C], BF16, name="ws_sb")
+        nc.sync.dma_start(out=ws_sb[:], in_=w_view)
+        load_h(0)
+        for g in range(NG):
+            load_m(g)
+        load_h(1)
+        for t in range(0, 4):
+            load_a(t)
+        load_h(2)
+        for t in range(4, 8):
+            load_a(t)
+        load_h(3)
+        for t in range(8, A_BUFS):
+            load_a(t)
+
+        def emit_transposes(pairs):
+            for dst, src in pairs:
+                nc.tensor.transpose(out=dst, in_=src, identity=ident[:])
+
+        bias_ps = ps_s.tile([P, C], F32, name="bias_ps", tag="s")
+        nc.tensor.matmul(out=bias_ps[:], lhsT=ones[:], rhs=brow[:], start=True, stop=True)
+        bias_bc = keep.tile([P, C], F32, name="bias_bc")
+        nc.vector.tensor_copy(out=bias_bc[:], in_=bias_ps[:])
+
+        ws_words = ws_sb[:].bitcast(F32)
+        wsT = {}
+        for u in range(2):
+            bank = ps_t.tile([P, 4, P], F32, name="wsT_ps%d" % u, tag="t")
+            emit_transposes(
+                [(bank[:, o, :], ws_words[:, o, u * P : (u + 1) * P]) for o in range(4)]
+            )
+            wsT[u] = keep.tile([P, C], F32, name="wsT%d" % u)
+            if u == 0:
+                nc.scalar.copy(out=wsT[u][:], in_=bank[:].rearrange("p o c -> p (o c)"))
+            else:
+                nc.vector.tensor_copy(out=wsT[u][:], in_=bank[:].rearrange("p o c -> p (o c)"))
+
+        hT = {}
+        th_bank = {}
+
+        def th_list(pair):
+            th_bank[pair] = ps_t.tile([P, 2, 2, P], F32, name="hT_ps%d" % pair, tag="t")
+            res = []
+            for tt in range(2):
+                t = 2 * pair + tt
+                words = h_sb[t // 4][:].bitcast(F32)
+                for u in range(2):
+                    res.append((th_bank[pair][:, tt, u, :], words[:, t % 4, u * P : (u + 1) * P]))
+            return res
+
+        def copy_h(pair):
+            hT[pair] = keep.tile([P, 2, 2, P], F32, name="hT%d" % pair)
+            nc.scalar.copy(out=hT[pair][:], in_=th_bank[pair][:])
+
+        ta_bank = {}
+        a_grp = {}
+        a_codes = {}
+        a_scales = {}
+
+        def ta_list(t):
+            words = a_sb[t][:].bitcast(F32)
+            res = []
+            for half in range(2):
+                ta_bank[(t, half)] = ps_t.tile(
+                    [P, 2, 2, P], F32, name="aT_ps%d_%d" % (t, half), tag="t"
+                )
+                for gg in range(2):
+                    for u in range(2):
+                        w0 = (2 * half + gg) * 256 + u * P
+                        res.append((ta_bank[(t, half)][:, gg, u, :], words[:, w0 : w0 + P]))
+            return res
+
+        def copy_a(t):
+            a_grp[t] = g_pool.tile([P, NG, P, 2], F32, name="agrp%d" % t, tag="g", align_bytes=64)
+            for half in range(2):
+                nc.scalar.copy(
+                    out=a_grp[t][:, 2 * half : 2 * half + 2, :, :],
+                    in_=ta_bank[(t, half)][:].rearrange("p g u i -> p g i u"),
+                )
+
+        def quant_a(t):
+            a_codes[t] = keep.tile([P, NG * P], U32, name="acod%d" % t, align_bytes=64)
+            a_scales[t] = keep.tile([P, NG * P], U8, name="ascl%d" % t, align_bytes=64)
+            nc.vector.quantize_mx(
+                out=a_codes[t][:].bitcast(FP8X4),
+                scales=a_scales[t][:],
+                in_=a_grp[t][:].rearrange("p g i u -> p (g i u)").bitcast(BF16),
+            )
+
+        m_grp = {}
+        m_codes = {}
+        m_scales = {}
+
+        def regroup_m(g, engine):
+            m_grp[g] = keep.tile([P, C, 4], BF16, name="mgrp%d" % g, align_bytes=64)
+            dst = m_grp[g][:].rearrange("p (c i) t -> p c t i", i=4)
+            src = (
+                m_raw[g][:]
+                .rearrange("p u (e c) -> p (u e) c", e=2)
+                .rearrange("p t (c i) -> p c t i", i=4)
+            )
+            if engine == "v":
+                nc.vector.tensor_copy(out=dst, in_=src)
+            else:
+                nc.scalar.copy(out=dst, in_=src)
+
+        def quant_m(g):
+            m_codes[g] = keep.tile([P, C], U32, name="mcod%d" % g, align_bytes=64)
+            m_scales[g] = keep.tile([P, C], U8, name="mscl%d" % g, align_bytes=64)
+            nc.vector.quantize_mx(
+                out=m_codes[g][:].bitcast(FP8X4),
+                scales=m_scales[g][:],
+                in_=m_grp[g][:].rearrange("p c t -> p (c t)"),
+            )
+
+        acc = {}
+        self_ps = {}
+        agg_ps = {}
+        ws_bf = {}
+        for u in range(2):
+            ws_bf[u] = wsT[u][:].bitcast(BF16).rearrange("p (c e) -> p c e", e=2)
+
+        def x_round(p_tile, t_pairs):
+            per = (len(t_pairs) + 3) // 4
+            if p_tile is None:
+                emit_transposes(t_pairs)
+                return
+            self_ps[p_tile] = ps_s.tile([P, C], F32, name="self%d" % p_tile, tag="s")
+            h_bf = hT[p_tile // 2][:].bitcast(BF16).rearrange("p t u (i e) -> p t u i e", e=2)
+            for q in range(4):
+                u, e = divmod(q, 2)
+                nc.tensor.matmul(
+                    out=self_ps[p_tile][:],
+                    lhsT=h_bf[:, p_tile % 2, u, :, e],
+                    rhs=ws_bf[u][:, :, e],
+                    start=(q == 0),
+                    stop=(q == 3),
+                )
+                emit_transposes(t_pairs[q * per : (q + 1) * per])
+
+        def self_out(t):
+            acc[t] = keep.tile([P, C], F32, name="acc%d" % t)
+            nc.vector.tensor_tensor(out=acc[t][:], in0=self_ps[t][:], in1=bias_bc[:], op=ADD)
+
+        def mx_round(t):
+            agg_ps[t] = ps_a.tile([P, C], F32, name="agg%d" % t, tag="m")
+            for g in range(NG):
+                nc.tensor.matmul_mx(
+                    out=agg_ps[t][:],
+                    lhsT=a_codes[t][:, g * P : (g + 1) * P].bitcast(FP8X4),
+                    lhsT_scale=a_scales[t][:, g * P : (g + 1) * P],
+                    rhs=m_codes[g][:].bitcast(FP8X4),
+                    rhs_scale=m_scales[g][:],
+                    start=(g == 0),
+                    stop=(g == NG - 1),
+                )
+
+        def agg_add(t):
+            nc.vector.tensor_tensor(out=acc[t][:], in0=agg_ps[t][:], in1=acc[t][:], op=ADD)
+
+        def relu_store(t, engine):
+            if engine == "v":
+                nc.vector.tensor_scalar_max(out=acc[t][:], in0=acc[t][:], scalar1=0.0)
+            else:
+                nc.scalar.activation(out=acc[t][:], in_=acc[t][:], func=RELU)
+            nc.sync.dma_start(out=o_view[:, t, :], in_=acc[t][:])
+
+        emit_transposes(th_list(0))
+        copy_h(0)
+        emit_transposes(th_list(1))
+        copy_h(1)
+        regroup_m(0, "s")
+        regroup_m(1, "s")
+
+        v_extra = {
+            0: [("r", 2)],
+            1: [("r", 3)],
+            2: [("q", 2), ("q", 0)],
+            3: [("q", 3), ("q", 1)],
+        }
+
+        for r in range(NT + LM):
+            ta = r - LA
+            mx = r - LM
+            has_ta = 0 <= ta < NT
+            pairs = []
+            if r == 3:
+                pairs = [2, 3]
+            elif r % 2 == 1 and 7 <= r <= 13:
+                pairs = [(r + 1) // 2]
+
+            ta_ops = ta_list(ta) if has_ta else []
+            th_ops = []
+            for pr in pairs:
+                th_ops.extend(th_list(pr))
+            if ta_ops and th_ops:
+                woven = []
+                for q in range(4):
+                    woven.extend(ta_ops[2 * q : 2 * q + 2])
+                    woven.append(th_ops[q])
+            else:
+                woven = ta_ops + th_ops
+            x_round(r if r < NT else None, woven)
+            if has_ta and ta + A_BUFS < NT:
+                load_a(ta + A_BUFS)
+
+            done_s = r - LM - 2
+            if done_s >= 0 and done_s % 2 == 0 and done_s < NT - 2:
+                relu_store(done_s, "s")
+            if has_ta:
+                copy_a(ta)
+            for pr in pairs:
+                copy_h(pr)
+            if r < NT:
+                self_out(r)
+            for kind, g in v_extra.get(r, []):
+                if kind == "r":
+                    regroup_m(g, "v")
+                else:
+                    quant_m(g)
+            done_v = r - LM - 1
+            if done_v >= 0 and done_v % 2 == 1 and done_v < NT - 2:
+                relu_store(done_v, "v")
+            if has_ta:
+                quant_a(ta)
+            if mx >= 0:
+                mx_round(mx)
+                agg_add(mx)
+                if mx == NT - 2:
+                    relu_store(mx, "s")
+                if mx == NT - 1:
+                    relu_store(mx, "v")

@@ -18,9 +18,15 @@ NT = NODES // P
 NG = NODES // 512
 FLOPS = 2 * NODES * NODES * C + 2 * NODES * C * C
 
-LA = 4
-LM = 6
 A_BUFS = 10
+FIRST_LOADS = [
+    ("h", 0), ("a", 0), ("h", 1), ("a", 1), ("a", 2), ("h", 2), ("a", 3), ("a", 4), ("h", 3),
+    ("a", 5), ("m", 0), ("a", 6), ("h", 4), ("a", 7), ("m", 1), ("a", 8), ("h", 5), ("a", 9),
+    ("m", 2),
+]
+LATE_LOADS = {0: ("h", 6), 1: ("m", 3), 2: ("h", 7)}
+V_EXTRA = {8: ("r", 0), 9: ("q", 0), 10: ("r", 1), 11: ("q", 1), 12: ("r", 2), 13: ("q", 2),
+           14: ("r", 3), 15: ("q", 3)}
 
 
 def tile_gcnstacking_pb_kernel(tc, A, msg, h, Ws, b, out):
@@ -36,9 +42,8 @@ def tile_gcnstacking_pb_kernel(tc, A, msg, h, Ws, b, out):
         keep = ctx.enter_context(tc.tile_pool(name="keep", bufs=1))
         a_pool = ctx.enter_context(tc.tile_pool(name="araw", bufs=A_BUFS))
         g_pool = ctx.enter_context(tc.tile_pool(name="agrp", bufs=3))
-        ps_t = ctx.enter_context(tc.psum_pool(name="pst", bufs=3))
+        ps_t = ctx.enter_context(tc.psum_pool(name="pst", bufs=5))
         ps_s = ctx.enter_context(tc.psum_pool(name="pss", bufs=3))
-        ps_a = ctx.enter_context(tc.psum_pool(name="psa", bufs=2))
         ctx.enter_context(tc.manual_schedule())
 
         ident = keep.tile([P, P], F32, name="ident")
@@ -61,8 +66,8 @@ def tile_gcnstacking_pb_kernel(tc, A, msg, h, Ws, b, out):
             nc.sync.dma_start(out=a_sb[t][:], in_=a_view[:, t, :])
 
         def load_h(q):
-            h_sb[q] = keep.tile([P, 4, C], BF16, name="h%d" % q)
-            nc.sync.dma_start(out=h_sb[q][:], in_=h_view[:, 4 * q : 4 * q + 4, :])
+            h_sb[q] = keep.tile([P, 2, C], BF16, name="h%d" % q)
+            nc.sync.dma_start(out=h_sb[q][:], in_=h_view[:, 2 * q : 2 * q + 2, :])
 
         def load_m(g):
             m_raw[g] = keep.tile([P, 2, 2 * C], BF16, name="mraw%d" % g)
@@ -70,27 +75,19 @@ def tile_gcnstacking_pb_kernel(tc, A, msg, h, Ws, b, out):
 
         ws_sb = keep.tile([P, 4, C], BF16, name="ws_sb")
         nc.sync.dma_start(out=ws_sb[:], in_=w_view)
-        load_h(0)
-        for g in range(NG):
-            load_m(g)
-        load_h(1)
-        for t in range(0, 4):
-            load_a(t)
-        load_h(2)
-        for t in range(4, 8):
-            load_a(t)
-        load_h(3)
-        for t in range(8, A_BUFS):
-            load_a(t)
+        for kind, idx in FIRST_LOADS:
+            if kind == "a":
+                load_a(idx)
+            elif kind == "h":
+                load_h(idx)
+            else:
+                load_m(idx)
 
         def emit_transposes(pairs):
             for dst, src in pairs:
                 nc.tensor.transpose(out=dst, in_=src, identity=ident[:])
 
-        bias_ps = ps_s.tile([P, C], F32, name="bias_ps", tag="s")
-        nc.tensor.matmul(out=bias_ps[:], lhsT=ones[:], rhs=brow[:], start=True, stop=True)
         bias_bc = keep.tile([P, C], F32, name="bias_bc")
-        nc.vector.tensor_copy(out=bias_bc[:], in_=bias_ps[:])
 
         ws_words = ws_sb[:].bitcast(F32)
         wsT = {}
@@ -112,10 +109,9 @@ def tile_gcnstacking_pb_kernel(tc, A, msg, h, Ws, b, out):
             th_bank[pair] = ps_t.tile([P, 2, 2, P], F32, name="hT_ps%d" % pair, tag="t")
             res = []
             for tt in range(2):
-                t = 2 * pair + tt
-                words = h_sb[t // 4][:].bitcast(F32)
+                words = h_sb[pair][:].bitcast(F32)
                 for u in range(2):
-                    res.append((th_bank[pair][:, tt, u, :], words[:, t % 4, u * P : (u + 1) * P]))
+                    res.append((th_bank[pair][:, tt, u, :], words[:, tt, u * P : (u + 1) * P]))
             return res
 
         def copy_h(pair):
@@ -213,7 +209,7 @@ def tile_gcnstacking_pb_kernel(tc, A, msg, h, Ws, b, out):
             nc.vector.tensor_tensor(out=acc[t][:], in0=self_ps[t][:], in1=bias_bc[:], op=ADD)
 
         def mx_round(t):
-            agg_ps[t] = ps_a.tile([P, C], F32, name="agg%d" % t, tag="m")
+            agg_ps[t] = ps_t.tile([P, C], F32, name="agg%d" % t, tag="t")
             for g in range(NG):
                 nc.tensor.matmul_mx(
                     out=agg_ps[t][:],
@@ -237,66 +233,45 @@ def tile_gcnstacking_pb_kernel(tc, A, msg, h, Ws, b, out):
 
         emit_transposes(th_list(0))
         copy_h(0)
-        emit_transposes(th_list(1))
-        copy_h(1)
-        regroup_m(0, "s")
-        regroup_m(1, "s")
 
-        v_extra = {
-            0: [("r", 2)],
-            1: [("r", 3)],
-            2: [("q", 2), ("q", 0)],
-            3: [("q", 3), ("q", 1)],
-        }
-
-        for r in range(NT + LM):
-            ta = r - LA
-            mx = r - LM
-            has_ta = 0 <= ta < NT
-            pairs = []
-            if r == 3:
-                pairs = [2, 3]
-            elif r % 2 == 1 and 7 <= r <= 13:
-                pairs = [(r + 1) // 2]
-
-            ta_ops = ta_list(ta) if has_ta else []
-            th_ops = []
-            for pr in pairs:
-                th_ops.extend(th_list(pr))
-            if ta_ops and th_ops:
+        for r in range(NT):
+            ta_ops = ta_list(r)
+            pair = (r + 1) // 2
+            if r % 2 == 1 and pair < NT // 2:
+                th_ops = th_list(pair)
                 woven = []
                 for q in range(4):
                     woven.extend(ta_ops[2 * q : 2 * q + 2])
                     woven.append(th_ops[q])
             else:
-                woven = ta_ops + th_ops
-            x_round(r if r < NT else None, woven)
-            if has_ta and ta + A_BUFS < NT:
-                load_a(ta + A_BUFS)
-
-            done_s = r - LM - 2
-            if done_s >= 0 and done_s % 2 == 0 and done_s < NT - 2:
-                relu_store(done_s, "s")
-            if has_ta:
-                copy_a(ta)
-            for pr in pairs:
-                copy_h(pr)
-            if r < NT:
-                self_out(r)
-            for kind, g in v_extra.get(r, []):
+                th_ops = []
+                woven = ta_ops
+            x_round(r, woven)
+            if r == 0:
+                bias_ps = ps_s.tile([P, C], F32, name="bias_ps", tag="s")
+                nc.tensor.matmul(out=bias_ps[:], lhsT=ones[:], rhs=brow[:], start=True, stop=True)
+                nc.vector.tensor_copy(out=bias_bc[:], in_=bias_ps[:])
+            if r + A_BUFS < NT:
+                load_a(r + A_BUFS)
+            if r in LATE_LOADS:
+                kind, idx = LATE_LOADS[r]
+                if kind == "h":
+                    load_h(idx)
+                else:
+                    load_m(idx)
+            copy_a(r)
+            if th_ops:
+                copy_h(pair)
+            self_out(r)
+            if r in V_EXTRA:
+                kind, g = V_EXTRA[r]
                 if kind == "r":
                     regroup_m(g, "v")
                 else:
                     quant_m(g)
-            done_v = r - LM - 1
-            if done_v >= 0 and done_v % 2 == 1 and done_v < NT - 2:
-                relu_store(done_v, "v")
-            if has_ta:
-                quant_a(ta)
-            if mx >= 0:
-                mx_round(mx)
-                agg_add(mx)
-                if mx == NT - 2:
-                    relu_store(mx, "s")
-                if mx == NT - 1:
-                    relu_store(mx, "v")
+            quant_a(r)
+
+        for t in range(NT):
+            mx_round(t)
+            agg_add(t)
+            relu_store(t, "s" if t < NT - 1 else "v")

@@ -18,15 +18,9 @@ NT = NODES // P
 NG = NODES // 512
 FLOPS = 2 * NODES * NODES * C + 2 * NODES * C * C
 
+LA = 4
+LM = 6
 A_BUFS = 10
-FIRST_LOADS = [
-    ("h", 0), ("a", 0), ("h", 1), ("a", 1), ("a", 2), ("h", 2), ("a", 3), ("a", 4), ("h", 3),
-    ("a", 5), ("m", 0), ("a", 6), ("h", 4), ("a", 7), ("m", 1), ("a", 8), ("h", 5), ("a", 9),
-    ("m", 2),
-]
-LATE_LOADS = {0: ("h", 6), 1: ("m", 3), 2: ("h", 7)}
-V_EXTRA = {8: ("r", 0), 9: ("q", 0), 10: ("r", 1), 11: ("q", 1), 12: ("r", 2), 13: ("q", 2),
-           14: ("r", 3), 15: ("q", 3)}
 
 
 def tile_gcnstacking_pb_kernel(tc, A, msg, h, Ws, b, out):
@@ -42,8 +36,9 @@ def tile_gcnstacking_pb_kernel(tc, A, msg, h, Ws, b, out):
         keep = ctx.enter_context(tc.tile_pool(name="keep", bufs=1))
         a_pool = ctx.enter_context(tc.tile_pool(name="araw", bufs=A_BUFS))
         g_pool = ctx.enter_context(tc.tile_pool(name="agrp", bufs=3))
-        ps_t = ctx.enter_context(tc.psum_pool(name="pst", bufs=5))
+        ps_t = ctx.enter_context(tc.psum_pool(name="pst", bufs=3))
         ps_s = ctx.enter_context(tc.psum_pool(name="pss", bufs=3))
+        ps_a = ctx.enter_context(tc.psum_pool(name="psa", bufs=2))
         ctx.enter_context(tc.manual_schedule())
 
         ident = keep.tile([P, P], F32, name="ident")
@@ -66,8 +61,8 @@ def tile_gcnstacking_pb_kernel(tc, A, msg, h, Ws, b, out):
             nc.sync.dma_start(out=a_sb[t][:], in_=a_view[:, t, :])
 
         def load_h(q):
-            h_sb[q] = keep.tile([P, 2, C], BF16, name="h%d" % q)
-            nc.sync.dma_start(out=h_sb[q][:], in_=h_view[:, 2 * q : 2 * q + 2, :])
+            h_sb[q] = keep.tile([P, 4, C], BF16, name="h%d" % q)
+            nc.sync.dma_start(out=h_sb[q][:], in_=h_view[:, 4 * q : 4 * q + 4, :])
 
         def load_m(g):
             m_raw[g] = keep.tile([P, 2, 2 * C], BF16, name="mraw%d" % g)
@@ -75,13 +70,18 @@ def tile_gcnstacking_pb_kernel(tc, A, msg, h, Ws, b, out):
 
         ws_sb = keep.tile([P, 4, C], BF16, name="ws_sb")
         nc.sync.dma_start(out=ws_sb[:], in_=w_view)
-        for kind, idx in FIRST_LOADS:
-            if kind == "a":
-                load_a(idx)
-            elif kind == "h":
-                load_h(idx)
-            else:
-                load_m(idx)
+        load_h(0)
+        for g in range(NG):
+            load_m(g)
+        load_h(1)
+        for t in range(0, 4):
+            load_a(t)
+        load_h(2)
+        for t in range(4, 8):
+            load_a(t)
+        load_h(3)
+        for t in range(8, A_BUFS):
+            load_a(t)
 
         def emit_transposes(pairs):
             for dst, src in pairs:
@@ -96,11 +96,14 @@ def tile_gcnstacking_pb_kernel(tc, A, msg, h, Ws, b, out):
             emit_transposes(
                 [(bank[:, o, :], ws_words[:, o, u * P : (u + 1) * P]) for o in range(4)]
             )
-            wsT[u] = keep.tile([P, C], F32, name="wsT%d" % u)
+            wsT[u] = keep.tile([P, 2, C], BF16, name="wsT%d" % u)
+            halves = (
+                bank[:].rearrange("p o c -> p (o c)").bitcast(BF16).rearrange("p (c e) -> p e c", e=2)
+            )
             if u == 0:
-                nc.scalar.copy(out=wsT[u][:], in_=bank[:].rearrange("p o c -> p (o c)"))
+                nc.scalar.copy(out=wsT[u][:], in_=halves)
             else:
-                nc.vector.tensor_copy(out=wsT[u][:], in_=bank[:].rearrange("p o c -> p (o c)"))
+                nc.vector.tensor_copy(out=wsT[u][:], in_=halves)
 
         hT = {}
         th_bank = {}
@@ -109,14 +112,24 @@ def tile_gcnstacking_pb_kernel(tc, A, msg, h, Ws, b, out):
             th_bank[pair] = ps_t.tile([P, 2, 2, P], F32, name="hT_ps%d" % pair, tag="t")
             res = []
             for tt in range(2):
-                words = h_sb[pair][:].bitcast(F32)
+                t = 2 * pair + tt
+                words = h_sb[t // 4][:].bitcast(F32)
                 for u in range(2):
-                    res.append((th_bank[pair][:, tt, u, :], words[:, tt, u * P : (u + 1) * P]))
+                    res.append((th_bank[pair][:, tt, u, :], words[:, t % 4, u * P : (u + 1) * P]))
             return res
 
-        def copy_h(pair):
-            hT[pair] = keep.tile([P, 2, 2, P], F32, name="hT%d" % pair)
-            nc.scalar.copy(out=hT[pair][:], in_=th_bank[pair][:])
+        def copy_h(pair, engine):
+            hT[pair] = keep.tile([P, 4, 2, P], BF16, name="hT%d" % pair)
+            halves = (
+                th_bank[pair][:]
+                .rearrange("p t u i -> p (t u i)")
+                .bitcast(BF16)
+                .rearrange("p (s i e) -> p s e i", s=4, e=2)
+            )
+            if engine == "v":
+                nc.vector.tensor_copy(out=hT[pair][:], in_=halves)
+            else:
+                nc.scalar.copy(out=hT[pair][:], in_=halves)
 
         ta_bank = {}
         a_grp = {}
@@ -182,9 +195,6 @@ def tile_gcnstacking_pb_kernel(tc, A, msg, h, Ws, b, out):
         acc = {}
         self_ps = {}
         agg_ps = {}
-        ws_bf = {}
-        for u in range(2):
-            ws_bf[u] = wsT[u][:].bitcast(BF16).rearrange("p (c e) -> p c e", e=2)
 
         def x_round(p_tile, t_pairs):
             per = (len(t_pairs) + 3) // 4
@@ -192,13 +202,12 @@ def tile_gcnstacking_pb_kernel(tc, A, msg, h, Ws, b, out):
                 emit_transposes(t_pairs)
                 return
             self_ps[p_tile] = ps_s.tile([P, C], F32, name="self%d" % p_tile, tag="s")
-            h_bf = hT[p_tile // 2][:].bitcast(BF16).rearrange("p t u (i e) -> p t u i e", e=2)
             for q in range(4):
                 u, e = divmod(q, 2)
                 nc.tensor.matmul(
                     out=self_ps[p_tile][:],
-                    lhsT=h_bf[:, p_tile % 2, u, :, e],
-                    rhs=ws_bf[u][:, :, e],
+                    lhsT=hT[p_tile // 2][:, 2 * (p_tile % 2) + u, e, :],
+                    rhs=wsT[u][:, e, :],
                     start=(q == 0),
                     stop=(q == 3),
                 )
@@ -209,7 +218,7 @@ def tile_gcnstacking_pb_kernel(tc, A, msg, h, Ws, b, out):
             nc.vector.tensor_tensor(out=acc[t][:], in0=self_ps[t][:], in1=bias_bc[:], op=ADD)
 
         def mx_round(t):
-            agg_ps[t] = ps_t.tile([P, C], F32, name="agg%d" % t, tag="t")
+            agg_ps[t] = ps_a.tile([P, C], F32, name="agg%d" % t, tag="m")
             for g in range(NG):
                 nc.tensor.matmul_mx(
                     out=agg_ps[t][:],
@@ -232,46 +241,71 @@ def tile_gcnstacking_pb_kernel(tc, A, msg, h, Ws, b, out):
             nc.sync.dma_start(out=o_view[:, t, :], in_=acc[t][:])
 
         emit_transposes(th_list(0))
-        copy_h(0)
+        copy_h(0, "s")
+        emit_transposes(th_list(1))
+        copy_h(1, "v")
+        regroup_m(0, "s")
+        regroup_m(1, "s")
 
-        for r in range(NT):
-            ta_ops = ta_list(r)
-            pair = (r + 1) // 2
-            if r % 2 == 1 and pair < NT // 2:
-                th_ops = th_list(pair)
+        v_extra = {
+            0: [("r", 2)],
+            1: [("r", 3)],
+            2: [("q", 2), ("q", 0)],
+            3: [("q", 3), ("q", 1)],
+        }
+
+        for r in range(NT + LM):
+            ta = r - LA
+            mx = r - LM
+            has_ta = 0 <= ta < NT
+            pairs = []
+            if r == 3:
+                pairs = [2, 3]
+            elif r % 2 == 1 and 7 <= r <= 13:
+                pairs = [(r + 1) // 2]
+
+            ta_ops = ta_list(ta) if has_ta else []
+            th_ops = []
+            for pr in pairs:
+                th_ops.extend(th_list(pr))
+            if ta_ops and th_ops:
                 woven = []
                 for q in range(4):
                     woven.extend(ta_ops[2 * q : 2 * q + 2])
                     woven.append(th_ops[q])
             else:
-                th_ops = []
-                woven = ta_ops
-            x_round(r, woven)
+                woven = ta_ops + th_ops
+            x_round(r if r < NT else None, woven)
             if r == 0:
                 bias_ps = ps_s.tile([P, C], F32, name="bias_ps", tag="s")
                 nc.tensor.matmul(out=bias_ps[:], lhsT=ones[:], rhs=brow[:], start=True, stop=True)
                 nc.vector.tensor_copy(out=bias_bc[:], in_=bias_ps[:])
-            if r + A_BUFS < NT:
-                load_a(r + A_BUFS)
-            if r in LATE_LOADS:
-                kind, idx = LATE_LOADS[r]
-                if kind == "h":
-                    load_h(idx)
-                else:
-                    load_m(idx)
-            copy_a(r)
-            if th_ops:
-                copy_h(pair)
-            self_out(r)
-            if r in V_EXTRA:
-                kind, g = V_EXTRA[r]
+            if has_ta and ta + A_BUFS < NT:
+                load_a(ta + A_BUFS)
+
+            done_s = r - LM - 2
+            if done_s >= 0 and done_s % 2 == 0 and done_s < NT - 2:
+                relu_store(done_s, "s")
+            if has_ta:
+                copy_a(ta)
+            for pr in pairs:
+                copy_h(pr, "s")
+            if r < NT:
+                self_out(r)
+            for kind, g in v_extra.get(r, []):
                 if kind == "r":
                     regroup_m(g, "v")
                 else:
                     quant_m(g)
-            quant_a(r)
-
-        for t in range(NT):
-            mx_round(t)
-            agg_add(t)
-            relu_store(t, "s" if t < NT - 1 else "v")
+            done_v = r - LM - 1
+            if done_v >= 0 and done_v % 2 == 1 and done_v < NT - 2:
+                relu_store(done_v, "v")
+            if has_ta:
+                quant_a(ta)
+            if mx >= 0:
+                mx_round(mx)
+                agg_add(mx)
+                if mx == NT - 2:
+                    relu_store(mx, "s")
+                if mx == NT - 1:
+                    relu_store(mx, "v")

@@ -18,8 +18,6 @@ NT = NODES // P
 NG = NODES // 512
 FLOPS = 2 * NODES * NODES * C + 2 * NODES * C * C
 
-LA = 4
-LM = 6
 A_BUFS = 10
 
 
@@ -35,9 +33,9 @@ def tile_gcnstacking_pb_kernel(tc, A, msg, h, Ws, b, out):
     with ExitStack() as ctx:
         keep = ctx.enter_context(tc.tile_pool(name="keep", bufs=1))
         a_pool = ctx.enter_context(tc.tile_pool(name="araw", bufs=A_BUFS))
-        g_pool = ctx.enter_context(tc.tile_pool(name="agrp", bufs=3))
-        ps_t = ctx.enter_context(tc.psum_pool(name="pst", bufs=3))
-        ps_s = ctx.enter_context(tc.psum_pool(name="pss", bufs=3))
+        g_pool = ctx.enter_context(tc.tile_pool(name="agrp", bufs=4))
+        ps_t = ctx.enter_context(tc.psum_pool(name="pst", bufs=4))
+        ps_s = ctx.enter_context(tc.psum_pool(name="pss", bufs=2))
         ps_a = ctx.enter_context(tc.psum_pool(name="psa", bufs=2))
         ctx.enter_context(tc.manual_schedule())
 
@@ -71,16 +69,12 @@ def tile_gcnstacking_pb_kernel(tc, A, msg, h, Ws, b, out):
         ws_sb = keep.tile([P, 4, C], BF16, name="ws_sb")
         nc.sync.dma_start(out=ws_sb[:], in_=w_view)
         load_h(0)
+        load_h(1)
         for g in range(NG):
             load_m(g)
-        load_h(1)
-        for t in range(0, 4):
-            load_a(t)
         load_h(2)
-        for t in range(4, 8):
-            load_a(t)
         load_h(3)
-        for t in range(8, A_BUFS):
+        for t in range(A_BUFS):
             load_a(t)
 
         def emit_transposes(pairs):
@@ -96,14 +90,11 @@ def tile_gcnstacking_pb_kernel(tc, A, msg, h, Ws, b, out):
             emit_transposes(
                 [(bank[:, o, :], ws_words[:, o, u * P : (u + 1) * P]) for o in range(4)]
             )
-            wsT[u] = keep.tile([P, 2, C], BF16, name="wsT%d" % u)
-            halves = (
-                bank[:].rearrange("p o c -> p (o c)").bitcast(BF16).rearrange("p (c e) -> p e c", e=2)
-            )
+            wsT[u] = keep.tile([P, C], F32, name="wsT%d" % u)
             if u == 0:
-                nc.scalar.copy(out=wsT[u][:], in_=halves)
+                nc.scalar.copy(out=wsT[u][:], in_=bank[:].rearrange("p o c -> p (o c)"))
             else:
-                nc.vector.tensor_copy(out=wsT[u][:], in_=halves)
+                nc.vector.tensor_copy(out=wsT[u][:], in_=bank[:].rearrange("p o c -> p (o c)"))
 
         hT = {}
         th_bank = {}
@@ -118,18 +109,9 @@ def tile_gcnstacking_pb_kernel(tc, A, msg, h, Ws, b, out):
                     res.append((th_bank[pair][:, tt, u, :], words[:, t % 4, u * P : (u + 1) * P]))
             return res
 
-        def copy_h(pair, engine):
-            hT[pair] = keep.tile([P, 4, 2, P], BF16, name="hT%d" % pair)
-            halves = (
-                th_bank[pair][:]
-                .rearrange("p t u i -> p (t u i)")
-                .bitcast(BF16)
-                .rearrange("p (s i e) -> p s e i", s=4, e=2)
-            )
-            if engine == "v":
-                nc.vector.tensor_copy(out=hT[pair][:], in_=halves)
-            else:
-                nc.scalar.copy(out=hT[pair][:], in_=halves)
+        def copy_h(pair):
+            hT[pair] = keep.tile([P, 2, 2, P], F32, name="hT%d" % pair)
+            nc.scalar.copy(out=hT[pair][:], in_=th_bank[pair][:])
 
         ta_bank = {}
         a_grp = {}
@@ -195,117 +177,127 @@ def tile_gcnstacking_pb_kernel(tc, A, msg, h, Ws, b, out):
         acc = {}
         self_ps = {}
         agg_ps = {}
+        ws_bf = {}
+        for u in range(2):
+            ws_bf[u] = wsT[u][:].bitcast(BF16).rearrange("p (c e) -> p c e", e=2)
 
-        def x_round(p_tile, t_pairs):
-            per = (len(t_pairs) + 3) // 4
-            if p_tile is None:
-                emit_transposes(t_pairs)
-                return
-            self_ps[p_tile] = ps_s.tile([P, C], F32, name="self%d" % p_tile, tag="s")
+        def p_round(t, pool):
+            self_ps[t] = pool.tile([P, C], F32, name="self%d" % t, tag="s")
+            h_bf = hT[t // 2][:].bitcast(BF16).rearrange("p t u (i e) -> p t u i e", e=2)
             for q in range(4):
                 u, e = divmod(q, 2)
                 nc.tensor.matmul(
-                    out=self_ps[p_tile][:],
-                    lhsT=hT[p_tile // 2][:, 2 * (p_tile % 2) + u, e, :],
-                    rhs=wsT[u][:, e, :],
+                    out=self_ps[t][:],
+                    lhsT=h_bf[:, t % 2, u, :, e],
+                    rhs=ws_bf[u][:, :, e],
                     start=(q == 0),
                     stop=(q == 3),
                 )
-                emit_transposes(t_pairs[q * per : (q + 1) * per])
 
         def self_out(t):
             acc[t] = keep.tile([P, C], F32, name="acc%d" % t)
             nc.vector.tensor_tensor(out=acc[t][:], in0=self_ps[t][:], in1=bias_bc[:], op=ADD)
 
-        def mx_round(t):
-            agg_ps[t] = ps_a.tile([P, C], F32, name="agg%d" % t, tag="m")
+        def mx_round(t, pool, c0, c1):
+            agg_ps[(t, c0)] = pool.tile([P, c1 - c0], F32, name="agg%d_%d" % (t, c0), tag="s")
             for g in range(NG):
                 nc.tensor.matmul_mx(
-                    out=agg_ps[t][:],
+                    out=agg_ps[(t, c0)][:],
                     lhsT=a_codes[t][:, g * P : (g + 1) * P].bitcast(FP8X4),
                     lhsT_scale=a_scales[t][:, g * P : (g + 1) * P],
-                    rhs=m_codes[g][:].bitcast(FP8X4),
-                    rhs_scale=m_scales[g][:],
+                    rhs=m_codes[g][:, c0:c1].bitcast(FP8X4),
+                    rhs_scale=m_scales[g][:, c0:c1],
                     start=(g == 0),
                     stop=(g == NG - 1),
                 )
 
-        def agg_add(t):
-            nc.vector.tensor_tensor(out=acc[t][:], in0=agg_ps[t][:], in1=acc[t][:], op=ADD)
+        def agg_add(t, c0, c1):
+            nc.vector.tensor_tensor(
+                out=acc[t][:, c0:c1], in0=agg_ps[(t, c0)][:], in1=acc[t][:, c0:c1], op=ADD
+            )
 
-        def relu_store(t, engine):
+        def relu_store(t, engine, c0, c1):
             if engine == "v":
-                nc.vector.tensor_scalar_max(out=acc[t][:], in0=acc[t][:], scalar1=0.0)
+                nc.vector.tensor_scalar_max(out=acc[t][:, c0:c1], in0=acc[t][:, c0:c1], scalar1=0.0)
             else:
-                nc.scalar.activation(out=acc[t][:], in_=acc[t][:], func=RELU)
-            nc.sync.dma_start(out=o_view[:, t, :], in_=acc[t][:])
+                nc.scalar.activation(out=acc[t][:, c0:c1], in_=acc[t][:, c0:c1], func=RELU)
+            nc.sync.dma_start(out=o_view[:, t, c0:c1], in_=acc[t][:, c0:c1])
 
-        emit_transposes(th_list(0))
-        copy_h(0, "s")
-        emit_transposes(th_list(1))
-        copy_h(1, "v")
+        def th_chunk(q):
+            for pr in (2 * q, 2 * q + 1):
+                emit_transposes(th_list(pr))
+            for pr in (2 * q, 2 * q + 1):
+                copy_h(pr)
+
+        def ta_pair(t):
+            for tt in (t, t + 1):
+                emit_transposes(ta_list(tt))
+            for tt in (t, t + 1):
+                if tt + A_BUFS < NT:
+                    load_a(tt + A_BUFS)
+            for tt in (t, t + 1):
+                copy_a(tt)
+
+        th_chunk(0)
+        th_chunk(1)
         regroup_m(0, "s")
         regroup_m(1, "s")
+        p_round(0, ps_s)
+        bias_ps = ps_a.tile([P, C], F32, name="bias_ps", tag="s")
+        nc.tensor.matmul(out=bias_ps[:], lhsT=ones[:], rhs=brow[:], start=True, stop=True)
+        nc.vector.tensor_copy(out=bias_bc[:], in_=bias_ps[:])
+        self_out(0)
+        p_round(1, ps_s)
+        self_out(1)
+        regroup_m(2, "v")
+        p_round(2, ps_a)
+        self_out(2)
+        p_round(3, ps_a)
+        self_out(3)
+        regroup_m(3, "v")
+        th_chunk(2)
+        p_round(4, ps_s)
+        self_out(4)
+        quant_m(0)
+        quant_m(1)
+        th_chunk(3)
+        p_round(5, ps_s)
+        self_out(5)
+        quant_m(2)
+        quant_m(3)
+        ta_pair(0)
+        p_round(6, ps_s)
+        self_out(6)
+        quant_a(0)
+        quant_a(1)
 
-        v_extra = {
-            0: [("r", 2)],
-            1: [("r", 3)],
-            2: [("q", 2), ("q", 0)],
-            3: [("q", 3), ("q", 1)],
-        }
+        for k in range(NT // 2 - 1):
+            if k >= 1:
+                relu_store(2 * k - 2, "s", 0, C)
+            p_round(7 + k, ps_s)
+            ta_pair(2 * k + 2)
+            if k >= 1:
+                relu_store(2 * k - 1, "v", 0, C)
+            self_out(7 + k)
+            quant_a(2 * k + 2)
+            mx_round(2 * k, ps_a, 0, C)
+            agg_add(2 * k, 0, C)
+            quant_a(2 * k + 3)
+            mx_round(2 * k + 1, ps_a, 0, C)
+            agg_add(2 * k + 1, 0, C)
 
-        for r in range(NT + LM):
-            ta = r - LA
-            mx = r - LM
-            has_ta = 0 <= ta < NT
-            pairs = []
-            if r == 3:
-                pairs = [2, 3]
-            elif r % 2 == 1 and 7 <= r <= 13:
-                pairs = [(r + 1) // 2]
-
-            ta_ops = ta_list(ta) if has_ta else []
-            th_ops = []
-            for pr in pairs:
-                th_ops.extend(th_list(pr))
-            if ta_ops and th_ops:
-                woven = []
-                for q in range(4):
-                    woven.extend(ta_ops[2 * q : 2 * q + 2])
-                    woven.append(th_ops[q])
-            else:
-                woven = ta_ops + th_ops
-            x_round(r if r < NT else None, woven)
-            if r == 0:
-                bias_ps = ps_s.tile([P, C], F32, name="bias_ps", tag="s")
-                nc.tensor.matmul(out=bias_ps[:], lhsT=ones[:], rhs=brow[:], start=True, stop=True)
-                nc.vector.tensor_copy(out=bias_bc[:], in_=bias_ps[:])
-            if has_ta and ta + A_BUFS < NT:
-                load_a(ta + A_BUFS)
-
-            done_s = r - LM - 2
-            if done_s >= 0 and done_s % 2 == 0 and done_s < NT - 2:
-                relu_store(done_s, "s")
-            if has_ta:
-                copy_a(ta)
-            for pr in pairs:
-                copy_h(pr, "s")
-            if r < NT:
-                self_out(r)
-            for kind, g in v_extra.get(r, []):
-                if kind == "r":
-                    regroup_m(g, "v")
-                else:
-                    quant_m(g)
-            done_v = r - LM - 1
-            if done_v >= 0 and done_v % 2 == 1 and done_v < NT - 2:
-                relu_store(done_v, "v")
-            if has_ta:
-                quant_a(ta)
-            if mx >= 0:
-                mx_round(mx)
-                agg_add(mx)
-                if mx == NT - 2:
-                    relu_store(mx, "s")
-                if mx == NT - 1:
-                    relu_store(mx, "v")
+        relu_store(NT - 4, "s", 0, C)
+        p_round(NT - 2, ps_s)
+        relu_store(NT - 3, "v", 0, C)
+        self_out(NT - 2)
+        p_round(NT - 1, ps_s)
+        self_out(NT - 1)
+        mx_round(NT - 2, ps_a, 0, C)
+        agg_add(NT - 2, 0, C)
+        relu_store(NT - 2, "s", 0, C)
+        mx_round(NT - 1, ps_a, 0, C // 2)
+        agg_add(NT - 1, 0, C // 2)
+        relu_store(NT - 1, "s", 0, C // 2)
+        mx_round(NT - 1, ps_s, C // 2, C)
+        agg_add(NT - 1, C // 2, C)
+        relu_store(NT - 1, "v", C // 2, C)

@@ -43,6 +43,8 @@ def tile_gcnstacking_pb_kernel(tc, A, msg, h, Ws, b, out):
         masks.make_identity(nc, ident[:])
         ones = keep.tile([P, P], BF16, name="ones")
         nc.vector.memset(ones[:], 1.0)
+        zrow = keep.tile([P, C], BF16, name="zrow")
+        nc.vector.memset(zrow[:], 0.0)
         brow = keep.tile([P, C], BF16, name="brow")
         nc.vector.memset(brow[:], 0.0)
         warm = keep.tile([P, 1], F32, name="warm")
@@ -83,6 +85,14 @@ def tile_gcnstacking_pb_kernel(tc, A, msg, h, Ws, b, out):
 
         bias_bc = keep.tile([P, C], F32, name="bias_bc")
 
+        warm_ps = ps_s.tile([P, C], F32, name="warm_ps", tag="s")
+
+        def dummy(n):
+            for i in range(n):
+                nc.tensor.matmul(out=warm_ps[:], lhsT=ones[:], rhs=zrow[:], start=True, stop=True)
+
+        dummy(5)
+
         ws_words = ws_sb[:].bitcast(F32)
         wsT = {}
         for u in range(2):
@@ -95,6 +105,8 @@ def tile_gcnstacking_pb_kernel(tc, A, msg, h, Ws, b, out):
                 nc.scalar.copy(out=wsT[u][:], in_=bank[:].rearrange("p o c -> p (o c)"))
             else:
                 nc.vector.tensor_copy(out=wsT[u][:], in_=bank[:].rearrange("p o c -> p (o c)"))
+
+        dummy(1)
 
         hT = {}
         th_bank = {}
@@ -181,7 +193,7 @@ def tile_gcnstacking_pb_kernel(tc, A, msg, h, Ws, b, out):
         for u in range(2):
             ws_bf[u] = wsT[u][:].bitcast(BF16).rearrange("p (c e) -> p c e", e=2)
 
-        def p_round(t, pool):
+        def p_round(t, pool, t_pairs):
             self_ps[t] = pool.tile([P, C], F32, name="self%d" % t, tag="s")
             h_bf = hT[t // 2][:].bitcast(BF16).rearrange("p t u (i e) -> p t u i e", e=2)
             for q in range(4):
@@ -193,6 +205,7 @@ def tile_gcnstacking_pb_kernel(tc, A, msg, h, Ws, b, out):
                     start=(q == 0),
                     stop=(q == 3),
                 )
+                emit_transposes(t_pairs[q : q + 1] if q < 3 else t_pairs[3:])
 
         def self_out(t):
             acc[t] = keep.tile([P, C], F32, name="acc%d" % t)
@@ -223,62 +236,67 @@ def tile_gcnstacking_pb_kernel(tc, A, msg, h, Ws, b, out):
                 nc.scalar.activation(out=acc[t][:, c0:c1], in_=acc[t][:, c0:c1], func=RELU)
             nc.sync.dma_start(out=o_view[:, t, c0:c1], in_=acc[t][:, c0:c1])
 
-        def th_chunk(q):
-            for pr in (2 * q, 2 * q + 1):
-                emit_transposes(th_list(pr))
-            for pr in (2 * q, 2 * q + 1):
-                copy_h(pr)
+        def ta_pair_ops(t):
+            return ta_list(t) + ta_list(t + 1)
 
-        def ta_pair(t):
-            for tt in (t, t + 1):
-                emit_transposes(ta_list(tt))
+        def after_ta_pair(t):
             for tt in (t, t + 1):
                 if tt + A_BUFS < NT:
                     load_a(tt + A_BUFS)
             for tt in (t, t + 1):
                 copy_a(tt)
 
-        th_chunk(0)
-        th_chunk(1)
+        emit_transposes(th_list(0) + th_list(1))
+        copy_h(0)
+        copy_h(1)
+        dummy(1)
         regroup_m(0, "s")
-        regroup_m(1, "s")
-        p_round(0, ps_s)
+        p_round(0, ps_s, th_list(2))
         bias_ps = ps_a.tile([P, C], F32, name="bias_ps", tag="s")
         nc.tensor.matmul(out=bias_ps[:], lhsT=ones[:], rhs=brow[:], start=True, stop=True)
         nc.vector.tensor_copy(out=bias_bc[:], in_=bias_ps[:])
         self_out(0)
-        p_round(1, ps_s)
+        p_round(1, ps_s, th_list(3))
         self_out(1)
-        regroup_m(2, "v")
-        p_round(2, ps_a)
+        copy_h(2)
+        copy_h(3)
+        regroup_m(1, "s")
+        p_round(2, ps_a, [])
         self_out(2)
-        p_round(3, ps_a)
-        self_out(3)
         regroup_m(3, "v")
-        th_chunk(2)
-        p_round(4, ps_s)
+        p_round(3, ps_a, [])
+        self_out(3)
+        p_round(4, ps_s, th_list(4))
         self_out(4)
+        copy_h(4)
         quant_m(0)
-        quant_m(1)
-        th_chunk(3)
-        p_round(5, ps_s)
+        regroup_m(2, "s")
+        p_round(5, ps_s, th_list(5))
         self_out(5)
-        quant_m(2)
-        quant_m(3)
-        ta_pair(0)
-        p_round(6, ps_s)
+        quant_m(1)
+        p_round(6, ps_a, th_list(6))
         self_out(6)
+        quant_m(3)
+        p_round(7, ps_a, th_list(7))
+        self_out(7)
+        copy_h(5)
+        copy_h(6)
+        copy_h(7)
+        quant_m(2)
+        p_round(8, ps_s, ta_pair_ops(0))
+        after_ta_pair(0)
+        self_out(8)
         quant_a(0)
         quant_a(1)
 
         for k in range(NT // 2 - 1):
             if k >= 1:
                 relu_store(2 * k - 2, "s", 0, C)
-            p_round(7 + k, ps_s)
-            ta_pair(2 * k + 2)
+            p_round(9 + k, ps_s, ta_pair_ops(2 * k + 2))
+            after_ta_pair(2 * k + 2)
             if k >= 1:
                 relu_store(2 * k - 1, "v", 0, C)
-            self_out(7 + k)
+            self_out(9 + k)
             quant_a(2 * k + 2)
             mx_round(2 * k, ps_a, 0, C)
             agg_add(2 * k, 0, C)
@@ -287,11 +305,7 @@ def tile_gcnstacking_pb_kernel(tc, A, msg, h, Ws, b, out):
             agg_add(2 * k + 1, 0, C)
 
         relu_store(NT - 4, "s", 0, C)
-        p_round(NT - 2, ps_s)
         relu_store(NT - 3, "v", 0, C)
-        self_out(NT - 2)
-        p_round(NT - 1, ps_s)
-        self_out(NT - 1)
         mx_round(NT - 2, ps_a, 0, C)
         agg_add(NT - 2, 0, C)
         relu_store(NT - 2, "s", 0, C)

@@ -41,12 +41,12 @@ def tile_gcnstacking_pb_kernel(tc, A, msg, h, Ws, b, out):
 
         ident = keep.tile([P, P], F32, name="ident")
         masks.make_identity(nc, ident[:])
+        brow = keep.tile([P, C], BF16, name="brow")
+        nc.vector.memset(brow[:], 0.0)
         ones = keep.tile([P, P], BF16, name="ones")
         nc.vector.memset(ones[:], 1.0)
         zrow = keep.tile([P, C], BF16, name="zrow")
         nc.vector.memset(zrow[:], 0.0)
-        brow = keep.tile([P, C], BF16, name="brow")
-        nc.vector.memset(brow[:], 0.0)
         warm = keep.tile([P, 1], F32, name="warm")
         nc.vector.memset(warm[:], 0.0)
         nc.scalar.dma_start(out=brow[0:1, :], in_=b_view)
@@ -252,16 +252,16 @@ def tile_gcnstacking_pb_kernel(tc, A, msg, h, Ws, b, out):
         dummy(1)
         regroup_m(0, "s")
         p_round(0, ps_s, th_list(2))
-        bias_ps = ps_a.tile([P, C], F32, name="bias_ps", tag="s")
-        nc.tensor.matmul(out=bias_ps[:], lhsT=ones[:], rhs=brow[:], start=True, stop=True)
-        nc.vector.tensor_copy(out=bias_bc[:], in_=bias_ps[:])
-        self_out(0)
         p_round(1, ps_s, th_list(3))
-        self_out(1)
         copy_h(2)
         copy_h(3)
         regroup_m(1, "s")
         p_round(2, ps_a, [])
+        bias_ps = ps_t.tile([P, C], F32, name="bias_ps", tag="t")
+        nc.tensor.matmul(out=bias_ps[:], lhsT=ones[:], rhs=brow[:], start=True, stop=True)
+        nc.vector.tensor_copy(out=bias_bc[:], in_=bias_ps[:])
+        self_out(0)
+        self_out(1)
         self_out(2)
         regroup_m(3, "v")
         p_round(3, ps_a, [])

@@ -9,6 +9,7 @@ U32 = mybir.dt.uint32
 U8 = mybir.dt.uint8
 FP8X4 = mybir.dt.float8_e4m3fn_x4
 ADD = mybir.AluOpType.add
+MULT = mybir.AluOpType.mult
 RELU = mybir.ActivationFunctionType.Relu
 
 P = 128
@@ -27,7 +28,7 @@ def tile_gcnstacking_pb_kernel(tc, A, msg, h, Ws, b, out):
     h_view = h.rearrange("b (p t) k -> p (b t) k", t=NT)
     o_view = out.rearrange("b (p t) c -> p (b t) c", t=NT)
     m_view = msg.rearrange("b (s p e) c -> p (b s) (e c)", s=2 * NG, p=P, e=2)
-    w_view = Ws.rearrange("(o p) k -> p o k", p=P)
+    w_view = Ws.rearrange("(p o) k -> p o k", p=P)
     b_view = b.rearrange("(o c) -> o c", o=1)
 
     with ExitStack() as ctx:
@@ -60,22 +61,29 @@ def tile_gcnstacking_pb_kernel(tc, A, msg, h, Ws, b, out):
             a_sb[t] = a_pool.tile([P, NODES], BF16, name="a%d" % t, tag="a")
             nc.sync.dma_start(out=a_sb[t][:], in_=a_view[:, t, :])
 
-        def load_h(q):
-            h_sb[q] = keep.tile([P, 4, C], BF16, name="h%d" % q)
-            nc.sync.dma_start(out=h_sb[q][:], in_=h_view[:, 4 * q : 4 * q + 4, :])
+        def load_h(t0, n):
+            tile = keep.tile([P, n, C], BF16, name="h%d" % t0)
+            nc.sync.dma_start(out=tile[:], in_=h_view[:, t0 : t0 + n, :])
+            for i in range(n):
+                h_sb[t0 + i] = tile[:, i, :]
 
         def load_m(g):
             m_raw[g] = keep.tile([P, 2, 2 * C], BF16, name="mraw%d" % g)
             nc.sync.dma_start(out=m_raw[g][:], in_=m_view[:, 2 * g : 2 * g + 2, :])
 
-        ws_sb = keep.tile([P, 4, C], BF16, name="ws_sb")
-        nc.sync.dma_start(out=ws_sb[:], in_=w_view)
-        load_h(0)
-        load_h(1)
-        for g in range(NG):
-            load_m(g)
-        load_h(2)
-        load_h(3)
+        load_h(0, 2)
+        ws_sb = {}
+        for half in range(2):
+            ws_sb[half] = keep.tile([P, 2, C], BF16, name="ws_sb%d" % half)
+            nc.sync.dma_start(out=ws_sb[half][:], in_=w_view[:, 2 * half : 2 * half + 2, :])
+        load_h(2, 2)
+        load_h(4, 4)
+        load_m(0)
+        load_m(1)
+        load_h(8, 4)
+        load_m(3)
+        load_m(2)
+        load_h(12, 4)
         for t in range(A_BUFS):
             load_a(t)
 
@@ -91,22 +99,23 @@ def tile_gcnstacking_pb_kernel(tc, A, msg, h, Ws, b, out):
             for i in range(n):
                 nc.tensor.matmul(out=warm_ps[:], lhsT=ones[:], rhs=zrow[:], start=True, stop=True)
 
-        dummy(5)
-
-        ws_words = ws_sb[:].bitcast(F32)
         wsT = {}
-        for u in range(2):
-            bank = ps_t.tile([P, 4, P], F32, name="wsT_ps%d" % u, tag="t")
-            emit_transposes(
-                [(bank[:, o, :], ws_words[:, o, u * P : (u + 1) * P]) for o in range(4)]
-            )
-            wsT[u] = keep.tile([P, C], F32, name="wsT%d" % u)
-            if u == 0:
-                nc.scalar.copy(out=wsT[u][:], in_=bank[:].rearrange("p o c -> p (o c)"))
-            else:
-                nc.vector.tensor_copy(out=wsT[u][:], in_=bank[:].rearrange("p o c -> p (o c)"))
 
-        dummy(1)
+        def transpose_ws():
+            bank = {}
+            for u in range(2):
+                bank[u] = ps_t.tile([P, 4, P], F32, name="wsT_ps%d" % u, tag="t")
+                wsT[u] = keep.tile([P, C], F32, name="wsT%d" % u)
+            for o in range(4):
+                words = ws_sb[o // 2][:].bitcast(F32)
+                emit_transposes(
+                    [(bank[u][:, o, :], words[:, o % 2, u * P : (u + 1) * P]) for u in range(2)]
+                )
+            for u, copy in ((0, nc.scalar.copy), (1, nc.vector.tensor_copy)):
+                copy(
+                    out=wsT[u][:].rearrange("p (c o) -> p c o", o=4),
+                    in_=bank[u][:].rearrange("p o c -> p c o"),
+                )
 
         hT = {}
         th_bank = {}
@@ -116,9 +125,9 @@ def tile_gcnstacking_pb_kernel(tc, A, msg, h, Ws, b, out):
             res = []
             for tt in range(2):
                 t = 2 * pair + tt
-                words = h_sb[t // 4][:].bitcast(F32)
+                words = h_sb[t].bitcast(F32)
                 for u in range(2):
-                    res.append((th_bank[pair][:, tt, u, :], words[:, t % 4, u * P : (u + 1) * P]))
+                    res.append((th_bank[pair][:, tt, u, :], words[:, u * P : (u + 1) * P]))
             return res
 
         def copy_h(pair):
@@ -174,6 +183,10 @@ def tile_gcnstacking_pb_kernel(tc, A, msg, h, Ws, b, out):
             )
             if engine == "v":
                 nc.vector.tensor_copy(out=dst, in_=src)
+            elif engine == "g":
+                nc.gpsimd.tensor_scalar(
+                    out=dst, in0=src, scalar1=1.0, scalar2=0.0, op0=MULT, op1=ADD
+                )
             else:
                 nc.scalar.copy(out=dst, in_=src)
 
@@ -190,8 +203,6 @@ def tile_gcnstacking_pb_kernel(tc, A, msg, h, Ws, b, out):
         self_ps = {}
         agg_ps = {}
         ws_bf = {}
-        for u in range(2):
-            ws_bf[u] = wsT[u][:].bitcast(BF16).rearrange("p (c e) -> p c e", e=2)
 
         def p_round(t, pool, t_pairs):
             self_ps[t] = pool.tile([P, C], F32, name="self%d" % t, tag="s")
@@ -246,48 +257,54 @@ def tile_gcnstacking_pb_kernel(tc, A, msg, h, Ws, b, out):
             for tt in (t, t + 1):
                 copy_a(tt)
 
-        emit_transposes(th_list(0) + th_list(1))
+        dummy(4)
+        emit_transposes(th_list(0))
         copy_h(0)
-        copy_h(1)
         dummy(1)
-        regroup_m(0, "s")
-        p_round(0, ps_s, th_list(2))
-        p_round(1, ps_s, th_list(3))
+        transpose_ws()
+        for u in range(2):
+            ws_bf[u] = wsT[u][:].bitcast(BF16).rearrange("p (c e) -> p c e", e=2)
+        dummy(2)
+        p_round(0, ps_s, th_list(1))
+        copy_h(1)
+        p_round(1, ps_s, th_list(2))
         copy_h(2)
-        copy_h(3)
-        regroup_m(1, "s")
-        p_round(2, ps_a, [])
+        regroup_m(0, "g")
         bias_ps = ps_t.tile([P, C], F32, name="bias_ps", tag="t")
         nc.tensor.matmul(out=bias_ps[:], lhsT=ones[:], rhs=brow[:], start=True, stop=True)
         nc.vector.tensor_copy(out=bias_bc[:], in_=bias_ps[:])
         self_out(0)
         self_out(1)
+        p_round(2, ps_a, th_list(3))
         self_out(2)
-        regroup_m(3, "v")
-        p_round(3, ps_a, [])
+        copy_h(3)
+        regroup_m(1, "v")
+        p_round(3, ps_a, th_list(4))
         self_out(3)
-        p_round(4, ps_s, th_list(4))
-        self_out(4)
         copy_h(4)
-        quant_m(0)
-        regroup_m(2, "s")
-        p_round(5, ps_s, th_list(5))
-        self_out(5)
         quant_m(1)
-        p_round(6, ps_a, th_list(6))
-        self_out(6)
-        quant_m(3)
-        p_round(7, ps_a, th_list(7))
-        self_out(7)
+        regroup_m(3, "v")
+        p_round(4, ps_s, th_list(5))
+        self_out(4)
         copy_h(5)
+        regroup_m(2, "s")
+        quant_m(3)
+        p_round(5, ps_s, th_list(6))
+        self_out(5)
+        quant_m(0)
+        p_round(6, ps_a, th_list(7))
+        self_out(6)
         copy_h(6)
         copy_h(7)
+        first_pair = ta_pair_ops(0)
+        p_round(7, ps_a, first_pair[:4])
         quant_m(2)
-        p_round(8, ps_s, ta_pair_ops(0))
+        p_round(8, ps_s, first_pair[4:])
         after_ta_pair(0)
-        self_out(8)
         quant_a(0)
+        self_out(7)
         quant_a(1)
+        self_out(8)
 
         for k in range(NT // 2 - 1):
             if k >= 1:

@@ -9,7 +9,6 @@ U32 = mybir.dt.uint32
 U8 = mybir.dt.uint8
 FP8X4 = mybir.dt.float8_e4m3fn_x4
 ADD = mybir.AluOpType.add
-MULT = mybir.AluOpType.mult
 RELU = mybir.ActivationFunctionType.Relu
 
 P = 128
@@ -183,10 +182,6 @@ def tile_gcnstacking_pb_kernel(tc, A, msg, h, Ws, b, out):
             )
             if engine == "v":
                 nc.vector.tensor_copy(out=dst, in_=src)
-            elif engine == "g":
-                nc.gpsimd.tensor_scalar(
-                    out=dst, in0=src, scalar1=1.0, scalar2=0.0, op0=MULT, op1=ADD
-                )
             else:
                 nc.scalar.copy(out=dst, in_=src)
 
@@ -269,7 +264,7 @@ def tile_gcnstacking_pb_kernel(tc, A, msg, h, Ws, b, out):
         copy_h(1)
         p_round(1, ps_s, th_list(2))
         copy_h(2)
-        regroup_m(0, "g")
+        regroup_m(0, "s")
         bias_ps = ps_t.tile([P, C], F32, name="bias_ps", tag="t")
         nc.tensor.matmul(out=bias_ps[:], lhsT=ones[:], rhs=brow[:], start=True, stop=True)
         nc.vector.tensor_copy(out=bias_bc[:], in_=bias_ps[:])

@@ -104,17 +104,19 @@ def tile_gcnstacking_pb_kernel(tc, A, msg, h, Ws, b, out):
             bank = {}
             for u in range(2):
                 bank[u] = ps_t.tile([P, 4, P], F32, name="wsT_ps%d" % u, tag="t")
-                wsT[u] = keep.tile([P, C], F32, name="wsT%d" % u)
+                wsT[u] = keep.tile([P, 2, C], BF16, name="wsT%d" % u)
             for o in range(4):
                 words = ws_sb[o // 2][:].bitcast(F32)
                 emit_transposes(
                     [(bank[u][:, o, :], words[:, o % 2, u * P : (u + 1) * P]) for u in range(2)]
                 )
             for u, copy in ((0, nc.scalar.copy), (1, nc.vector.tensor_copy)):
-                copy(
-                    out=wsT[u][:].rearrange("p (c o) -> p c o", o=4),
-                    in_=bank[u][:].rearrange("p o c -> p c o"),
-                )
+                pairs = bank[u][:].rearrange("p o c -> p (o c)").bitcast(BF16)
+                for e in range(2):
+                    copy(
+                        out=wsT[u][:, e, :].rearrange("p (c o) -> p c o", o=4),
+                        in_=pairs.rearrange("p (o c e) -> p e c o", o=4, e=2)[:, e, :, :],
+                    )
 
         hT = {}
         th_bank = {}
@@ -197,7 +199,6 @@ def tile_gcnstacking_pb_kernel(tc, A, msg, h, Ws, b, out):
         acc = {}
         self_ps = {}
         agg_ps = {}
-        ws_bf = {}
 
         def p_round(t, pool, t_pairs):
             self_ps[t] = pool.tile([P, C], F32, name="self%d" % t, tag="s")
@@ -207,7 +208,7 @@ def tile_gcnstacking_pb_kernel(tc, A, msg, h, Ws, b, out):
                 nc.tensor.matmul(
                     out=self_ps[t][:],
                     lhsT=h_bf[:, t % 2, u, :, e],
-                    rhs=ws_bf[u][:, :, e],
+                    rhs=wsT[u][:, e, :],
                     start=(q == 0),
                     stop=(q == 3),
                 )
@@ -257,8 +258,6 @@ def tile_gcnstacking_pb_kernel(tc, A, msg, h, Ws, b, out):
         copy_h(0)
         dummy(1)
         transpose_ws()
-        for u in range(2):
-            ws_bf[u] = wsT[u][:].bitcast(BF16).rearrange("p (c e) -> p c e", e=2)
         dummy(2)
         p_round(0, ps_s, th_list(1))
         copy_h(1)

@@ -9,6 +9,7 @@ U32 = mybir.dt.uint32
 U8 = mybir.dt.uint8
 FP8X4 = mybir.dt.float8_e4m3fn_x4
 ADD = mybir.AluOpType.add
+MULT = mybir.AluOpType.mult
 RELU = mybir.ActivationFunctionType.Relu
 
 P = 128
@@ -78,12 +79,13 @@ def tile_gcnstacking_pb_kernel(tc, A, msg, h, Ws, b, out):
         load_h(2, 2)
         load_h(4, 4)
         load_m(0)
-        load_m(1)
         load_h(8, 4)
-        load_m(3)
-        load_m(2)
+        load_m(1)
         load_h(12, 4)
-        for t in range(A_BUFS):
+        load_m(3)
+        load_a(0)
+        load_m(2)
+        for t in range(1, A_BUFS):
             load_a(t)
 
         def emit_transposes(pairs):
@@ -184,6 +186,10 @@ def tile_gcnstacking_pb_kernel(tc, A, msg, h, Ws, b, out):
             )
             if engine == "v":
                 nc.vector.tensor_copy(out=dst, in_=src)
+            elif engine == "g":
+                nc.gpsimd.tensor_scalar(
+                    out=dst, in0=src, scalar1=1.0, scalar2=0.0, op0=MULT, op1=ADD
+                )
             else:
                 nc.scalar.copy(out=dst, in_=src)
 
@@ -263,7 +269,7 @@ def tile_gcnstacking_pb_kernel(tc, A, msg, h, Ws, b, out):
         copy_h(1)
         p_round(1, ps_s, th_list(2))
         copy_h(2)
-        regroup_m(0, "s")
+        regroup_m(0, "g")
         bias_ps = ps_t.tile([P, C], F32, name="bias_ps", tag="t")
         nc.tensor.matmul(out=bias_ps[:], lhsT=ones[:], rhs=brow[:], start=True, stop=True)
         nc.vector.tensor_copy(out=bias_bc[:], in_=bias_ps[:])
@@ -277,12 +283,10 @@ def tile_gcnstacking_pb_kernel(tc, A, msg, h, Ws, b, out):
         self_out(3)
         copy_h(4)
         quant_m(1)
-        regroup_m(3, "v")
         p_round(4, ps_s, th_list(5))
         self_out(4)
         copy_h(5)
-        regroup_m(2, "s")
-        quant_m(3)
+        regroup_m(3, "s")
         p_round(5, ps_s, th_list(6))
         self_out(5)
         quant_m(0)
@@ -290,24 +294,32 @@ def tile_gcnstacking_pb_kernel(tc, A, msg, h, Ws, b, out):
         self_out(6)
         copy_h(6)
         copy_h(7)
-        first_pair = ta_pair_ops(0)
-        p_round(7, ps_a, first_pair[:4])
+        first_tile = ta_list(0)
+        p_round(7, ps_a, first_tile[:4])
+        quant_m(3)
+        self_out(7)
+        p_round(8, ps_s, first_tile[4:])
+        self_out(8)
+        regroup_m(2, "v")
         quant_m(2)
-        p_round(8, ps_s, first_pair[4:])
+        p_round(9, ps_s, ta_list(1))
         after_ta_pair(0)
         quant_a(0)
-        self_out(7)
+        self_out(9)
         quant_a(1)
-        self_out(8)
 
         for k in range(NT // 2 - 1):
             if k >= 1:
                 relu_store(2 * k - 2, "s", 0, C)
-            p_round(9 + k, ps_s, ta_pair_ops(2 * k + 2))
+            if 10 + k < NT:
+                p_round(10 + k, ps_s, ta_pair_ops(2 * k + 2))
+            else:
+                emit_transposes(ta_pair_ops(2 * k + 2))
             after_ta_pair(2 * k + 2)
             if k >= 1:
                 relu_store(2 * k - 1, "v", 0, C)
-            self_out(9 + k)
+            if 10 + k < NT:
+                self_out(10 + k)
             quant_a(2 * k + 2)
             mx_round(2 * k, ps_a, 0, C)
             agg_add(2 * k, 0, C)

from contextlib import ExitStack

import concourse.masks as masks
import concourse.mybir as mybir

F32 = mybir.dt.float32
BF16 = mybir.dt.bfloat16
U32 = mybir.dt.uint32
U8 = mybir.dt.uint8
FP8X4 = mybir.dt.float8_e4m3fn_x4
ADD = mybir.AluOpType.add
MULT = mybir.AluOpType.mult
RELU = mybir.ActivationFunctionType.Relu

P = 128
NODES = 2048
C = 512
NT = NODES // P
NG = NODES // 512
FLOPS = 2 * NODES * NODES * C + 2 * NODES * C * C

A_BUFS = 10


def tile_gcnstacking_pb_kernel(tc, A, msg, h, Ws, b, out):
    nc = tc.nc
    a_view = A.rearrange("b (p t) j -> p (b t) j", t=NT)
    h_view = h.rearrange("b (p t) k -> p (b t) k", t=NT)
    o_view = out.rearrange("b (p t) c -> p (b t) c", t=NT)
    m_view = msg.rearrange("b (s p e) c -> p (b s) (e c)", s=2 * NG, p=P, e=2)
    w_view = Ws.rearrange("(p o) k -> p o k", p=P)
    b_view = b.rearrange("(o c) -> o c", o=1)

    with ExitStack() as ctx:
        keep = ctx.enter_context(tc.tile_pool(name="keep", bufs=1))
        a_pool = ctx.enter_context(tc.tile_pool(name="araw", bufs=A_BUFS))
        g_pool = ctx.enter_context(tc.tile_pool(name="agrp", bufs=4))
        ps_t = ctx.enter_context(tc.psum_pool(name="pst", bufs=4))
        ps_s = ctx.enter_context(tc.psum_pool(name="pss", bufs=2))
        ps_a = ctx.enter_context(tc.psum_pool(name="psa", bufs=2))
        ctx.enter_context(tc.manual_schedule())

        ident = keep.tile([P, P], F32, name="ident")
        masks.make_identity(nc, ident[:])
        brow = keep.tile([P, C], BF16, name="brow")
        nc.vector.memset(brow[:], 0.0)
        ones = keep.tile([P, P], BF16, name="ones")
        nc.vector.memset(ones[:], 1.0)
        zrow = keep.tile([P, C], BF16, name="zrow")
        nc.vector.memset(zrow[:], 0.0)
        warm = keep.tile([P, 1], F32, name="warm")
        nc.vector.memset(warm[:], 0.0)
        nc.scalar.dma_start(out=brow[0:1, :], in_=b_view)
        nc.scalar.activation(out=warm[:], in_=warm[:], func=RELU)

        a_sb = {}
        h_sb = {}
        m_raw = {}

        def load_a(t):
            a_sb[t] = a_pool.tile([P, NODES], BF16, name="a%d" % t, tag="a")
            nc.sync.dma_start(out=a_sb[t][:], in_=a_view[:, t, :])

        def load_h(t0, n):
            tile = keep.tile([P, n, C], BF16, name="h%d" % t0)
            nc.sync.dma_start(out=tile[:], in_=h_view[:, t0 : t0 + n, :])
            for i in range(n):
                h_sb[t0 + i] = tile[:, i, :]

        def load_m(g):
            m_raw[g] = keep.tile([P, 2, 2 * C], BF16, name="mraw%d" % g)
            nc.sync.dma_start(out=m_raw[g][:], in_=m_view[:, 2 * g : 2 * g + 2, :])

        load_h(0, 2)
        ws_sb = {}
        for half in range(2):
            ws_sb[half] = keep.tile([P, 2, C], BF16, name="ws_sb%d" % half)
            nc.sync.dma_start(out=ws_sb[half][:], in_=w_view[:, 2 * half : 2 * half + 2, :])
        load_h(2, 2)
        load_h(4, 4)
        load_m(0)
        load_h(8, 4)
        load_m(1)
        load_h(12, 4)
        load_m(3)
        load_a(0)
        load_m(2)
        for t in range(1, A_BUFS):
            load_a(t)

        def emit_transposes(pairs):
            for dst, src in pairs:
                nc.tensor.transpose(out=dst, in_=src, identity=ident[:])

        bias_bc = keep.tile([P, C], F32, name="bias_bc")

        warm_ps = ps_s.tile([P, C], F32, name="warm_ps", tag="s")

        def dummy(n):
            for i in range(n):
                nc.tensor.matmul(out=warm_ps[:], lhsT=ones[:], rhs=zrow[:], start=True, stop=True)

        wsT = {}

        def transpose_ws():
            bank = {}
            for u in range(2):
                bank[u] = ps_t.tile([P, 4, P], F32, name="wsT_ps%d" % u, tag="t")
                wsT[u] = keep.tile([P, 2, C], BF16, name="wsT%d" % u)
            for o in range(4):
                words = ws_sb[o // 2][:].bitcast(F32)
                emit_transposes(
                    [(bank[u][:, o, :], words[:, o % 2, u * P : (u + 1) * P]) for u in range(2)]
                )
            for u, copy in ((0, nc.scalar.copy), (1, nc.vector.tensor_copy)):
                pairs = bank[u][:].rearrange("p o c -> p (o c)").bitcast(BF16)
                for e in range(2):
                    copy(
                        out=wsT[u][:, e, :].rearrange("p (c o) -> p c o", o=4),
                        in_=pairs.rearrange("p (o c e) -> p e c o", o=4, e=2)[:, e, :, :],
                    )

        hT = {}
        th_bank = {}

        def th_list(pair):
            th_bank[pair] = ps_t.tile([P, 2, 2, P], F32, name="hT_ps%d" % pair, tag="t")
            res = []
            for tt in range(2):
                t = 2 * pair + tt
                words = h_sb[t].bitcast(F32)
                for u in range(2):
                    res.append((th_bank[pair][:, tt, u, :], words[:, u * P : (u + 1) * P]))
            return res

        def copy_h(pair):
            hT[pair] = keep.tile([P, 2, 2, P], F32, name="hT%d" % pair)
            nc.scalar.copy(out=hT[pair][:], in_=th_bank[pair][:])

        ta_bank = {}
        a_grp = {}
        a_codes = {}
        a_scales = {}

        def ta_list(t):
            words = a_sb[t][:].bitcast(F32)
            res = []
            for half in range(2):
                ta_bank[(t, half)] = ps_t.tile(
                    [P, 2, 2, P], F32, name="aT_ps%d_%d" % (t, half), tag="t"
                )
                for gg in range(2):
                    for u in range(2):
                        w0 = (2 * half + gg) * 256 + u * P
                        res.append((ta_bank[(t, half)][:, gg, u, :], words[:, w0 : w0 + P]))
            return res

        def copy_a(t):
            a_grp[t] = g_pool.tile([P, NG, P, 2], F32, name="agrp%d" % t, tag="g", align_bytes=64)
            for half in range(2):
                nc.scalar.copy(
                    out=a_grp[t][:, 2 * half : 2 * half + 2, :, :],
                    in_=ta_bank[(t, half)][:].rearrange("p g u i -> p g i u"),
                )

        def quant_a(t):
            a_codes[t] = keep.tile([P, NG * P], U32, name="acod%d" % t, align_bytes=64)
            a_scales[t] = keep.tile([P, NG * P], U8, name="ascl%d" % t, align_bytes=64)
            nc.vector.quantize_mx(
                out=a_codes[t][:].bitcast(FP8X4),
                scales=a_scales[t][:],
                in_=a_grp[t][:].rearrange("p g i u -> p (g i u)").bitcast(BF16),
            )

        m_grp = {}
        m_codes = {}
        m_scales = {}

        def regroup_m(g, engine):
            m_grp[g] = keep.tile([P, C, 4], BF16, name="mgrp%d" % g, align_bytes=64)
            dst = m_grp[g][:].rearrange("p (c i) t -> p c t i", i=4)
            src = (
                m_raw[g][:]
                .rearrange("p u (e c) -> p (u e) c", e=2)
                .rearrange("p t (c i) -> p c t i", i=4)
            )
            if engine == "v":
                nc.vector.tensor_copy(out=dst, in_=src)
            elif engine == "g":
                nc.gpsimd.tensor_scalar(
                    out=dst, in0=src, scalar1=1.0, scalar2=0.0, op0=MULT, op1=ADD
                )
            else:
                nc.scalar.copy(out=dst, in_=src)

        def quant_m(g):
            m_codes[g] = keep.tile([P, C], U32, name="mcod%d" % g, align_bytes=64)
            m_scales[g] = keep.tile([P, C], U8, name="mscl%d" % g, align_bytes=64)
            nc.vector.quantize_mx(
                out=m_codes[g][:].bitcast(FP8X4),
                scales=m_scales[g][:],
                in_=m_grp[g][:].rearrange("p c t -> p (c t)"),
            )

        acc = {}
        self_ps = {}
        agg_ps = {}

        def p_round(t, pool, t_pairs):
            self_ps[t] = pool.tile([P, C], F32, name="self%d" % t, tag="s")
            h_bf = hT[t // 2][:].bitcast(BF16).rearrange("p t u (i e) -> p t u i e", e=2)
            for q in range(4):
                u, e = divmod(q, 2)
                nc.tensor.matmul(
                    out=self_ps[t][:],
                    lhsT=h_bf[:, t % 2, u, :, e],
                    rhs=wsT[u][:, e, :],
                    start=(q == 0),
                    stop=(q == 3),
                )
                emit_transposes(t_pairs[q : q + 1] if q < 3 else t_pairs[3:])

        def self_out(t):
            acc[t] = keep.tile([P, C], F32, name="acc%d" % t)
            nc.vector.tensor_tensor(out=acc[t][:], in0=self_ps[t][:], in1=bias_bc[:], op=ADD)

        def mx_round(t, pool, c0, c1):
            agg_ps[(t, c0)] = pool.tile([P, c1 - c0], F32, name="agg%d_%d" % (t, c0), tag="s")
            for g in range(NG):
                nc.tensor.matmul_mx(
                    out=agg_ps[(t, c0)][:],
                    lhsT=a_codes[t][:, g * P : (g + 1) * P].bitcast(FP8X4),
                    lhsT_scale=a_scales[t][:, g * P : (g + 1) * P],
                    rhs=m_codes[g][:, c0:c1].bitcast(FP8X4),
                    rhs_scale=m_scales[g][:, c0:c1],
                    start=(g == 0),
                    stop=(g == NG - 1),
                )

        def agg_add(t, c0, c1):
            nc.vector.tensor_tensor(
                out=acc[t][:, c0:c1], in0=agg_ps[(t, c0)][:], in1=acc[t][:, c0:c1], op=ADD
            )

        def relu_store(t, engine, c0, c1):
            if engine == "v":
                nc.vector.tensor_scalar_max(out=acc[t][:, c0:c1], in0=acc[t][:, c0:c1], scalar1=0.0)
            else:
                nc.scalar.activation(out=acc[t][:, c0:c1], in_=acc[t][:, c0:c1], func=RELU)
            nc.sync.dma_start(out=o_view[:, t, c0:c1], in_=acc[t][:, c0:c1])

        def ta_pair_ops(t):
            return ta_list(t) + ta_list(t + 1)

        def after_ta_pair(t):
            for tt in (t, t + 1):
                if tt + A_BUFS < NT:
                    load_a(tt + A_BUFS)
            for tt in (t, t + 1):
                copy_a(tt)

        dummy(4)
        emit_transposes(th_list(0))
        copy_h(0)
        dummy(1)
        transpose_ws()
        dummy(2)
        p_round(0, ps_s, th_list(1))
        copy_h(1)
        p_round(1, ps_s, th_list(2))
        copy_h(2)
        regroup_m(0, "g")
        bias_ps = ps_t.tile([P, C], F32, name="bias_ps", tag="t")
        nc.tensor.matmul(out=bias_ps[:], lhsT=ones[:], rhs=brow[:], start=True, stop=True)
        nc.vector.tensor_copy(out=bias_bc[:], in_=bias_ps[:])
        self_out(0)
        self_out(1)
        p_round(2, ps_a, th_list(3))
        self_out(2)
        copy_h(3)
        regroup_m(1, "v")
        p_round(3, ps_a, th_list(4))
        self_out(3)
        copy_h(4)
        quant_m(1)
        p_round(4, ps_s, th_list(5))
        self_out(4)
        copy_h(5)
        regroup_m(3, "s")
        p_round(5, ps_s, th_list(6))
        self_out(5)
        quant_m(0)
        p_round(6, ps_a, th_list(7))
        self_out(6)
        copy_h(6)
        copy_h(7)
        first_tile = ta_list(0)
        p_round(7, ps_a, first_tile[:4])
        quant_m(3)
        self_out(7)
        p_round(8, ps_s, first_tile[4:])
        self_out(8)
        regroup_m(2, "v")
        quant_m(2)
        p_round(9, ps_s, ta_list(1))
        after_ta_pair(0)
        quant_a(0)
        self_out(9)
        quant_a(1)

        for k in range(NT // 2 - 1):
            if k >= 1:
                relu_store(2 * k - 2, "s", 0, C)
            if 10 + k < NT:
                p_round(10 + k, ps_s, ta_pair_ops(2 * k + 2))
            else:
                emit_transposes(ta_pair_ops(2 * k + 2))
            after_ta_pair(2 * k + 2)
            if k >= 1:
                relu_store(2 * k - 1, "v", 0, C)
            if 10 + k < NT:
                self_out(10 + k)
            quant_a(2 * k + 2)
            mx_round(2 * k, ps_a, 0, C)
            agg_add(2 * k, 0, C)
            quant_a(2 * k + 3)
            mx_round(2 * k + 1, ps_a, 0, C)
            agg_add(2 * k + 1, 0, C)

        relu_store(NT - 4, "s", 0, C)
        relu_store(NT - 3, "v", 0, C)
        mx_round(NT - 2, ps_a, 0, C)
        agg_add(NT - 2, 0, C)
        relu_store(NT - 2, "s", 0, C)
        mx_round(NT - 1, ps_a, 0, C // 2)
        agg_add(NT - 1, 0, C // 2)
        relu_store(NT - 1, "s", 0, C // 2)
        mx_round(NT - 1, ps_s, C // 2, C)
        agg_add(NT - 1, C // 2, C)
        relu_store(NT - 1, "v", C // 2, C)
